import numpy as np
import ml_dtypes


def mxq(x, axis, fmt="e4m3"):
    dtype, down = {"e4m3": (ml_dtypes.float8_e4m3fn, 7), "e5m2": (ml_dtypes.float8_e5m2, 14)}[fmt]
    v = np.moveaxis(np.asarray(x, np.float32).astype(ml_dtypes.bfloat16).astype(np.float64), axis, -1)
    blocks = v.reshape(v.shape[:-1] + (-1, 32))
    amax = np.abs(blocks).max(-1, keepdims=True)
    byte = np.maximum(np.where(amax > 0, np.frexp(amax)[1] - 1 + 127, 0) - down, 1)
    scale = np.exp2(byte - 127.0)
    codes = (blocks / scale).astype(np.float32).astype(dtype).astype(np.float64)
    return np.moveaxis((codes * scale).reshape(v.shape), -1, axis)


WIDE = False


def mx_kscale(k):
    if not WIDE:
        return np.ones(k)
    levels = np.array([10, -10, 5, -5, 0])
    a = np.random.permutation(np.resize(levels, k // 512 * 4)).reshape(k // 512, 4)
    idx = np.arange(k)
    return np.exp2(a[idx // 512, idx % 128 // 32])


BF16 = ml_dtypes.bfloat16


def bf(x):
    return np.asarray(x, np.float32).astype(BF16)


def f64(x):
    return np.asarray(x).astype(np.float64)


E2M1 = np.array([0.0, 0.5, 1.0, 1.5, 2.0, 3.0, 4.0, 6.0, -0.0, -0.5, -1.0, -1.5, -2.0, -3.0, -4.0, -6.0])


def pack_weight(w, fmt):
    k, n = w.shape
    w = f64(bf(w)).reshape(k // 32, 32, n)
    amax = np.abs(w).max(1)
    if fmt == "e4m3":
        byte = np.frexp(amax)[1] - 1 + 127 - 7
    else:
        mant, ex = np.frexp(amax / 6.0)
        byte = np.where(mant > 0.5, ex, ex - 1) + 127
    byte = np.clip(np.where(amax > 0, byte, 1), 1, 254)
    scaled = (w * np.exp2(127.0 - byte)[:, None, :]).reshape(k, n).astype(np.float32)
    by_word = np.ascontiguousarray(scaled.reshape(k // 512, 128, 4, n).transpose(0, 1, 3, 2))
    if fmt == "e4m3":
        words = by_word.astype(ml_dtypes.float8_e4m3fn).view(np.uint8)
    else:
        c = by_word.astype(ml_dtypes.float4_e2m1fn).view(np.uint8) & 0xF
        words = c[..., 0::2] | (c[..., 1::2] << 4)
    return np.ascontiguousarray(words), np.ascontiguousarray(byte.astype(np.uint8).reshape(k // 512, 16, n))


def unpack_weight(words, scales, fmt):
    g, p, n, _ = words.shape
    if fmt == "e4m3":
        vals = np.ascontiguousarray(words).view(ml_dtypes.float8_e4m3fn).astype(np.float64)
    else:
        nib = np.empty((g, p, n, 4), np.uint8)
        nib[..., 0::2] = words & 0xF
        nib[..., 1::2] = words >> 4
        vals = E2M1[nib]
    vals = vals * np.repeat(np.exp2(scales.astype(np.float64) - 127.0), 8, axis=1)[..., None]
    return vals.transpose(0, 1, 3, 2).reshape(g * 512, n)


M, IN, OUT, R = 256, 4096, 4096, 128


def setup_inputs():
    s = mx_kscale(IN)
    x = np.random.standard_normal((M, IN)) * s
    w = np.random.standard_normal((IN, OUT)) * 0.0156 / s[:, None]
    w_lr = np.random.standard_normal((OUT, R)) * 0.06 / s[None, :R]
    weight_words, weight_scales = pack_weight(w, "e4m3")
    return {"x": bf(x), "weight_words": weight_words, "weight_scales": weight_scales, "low_rank_weight": bf(w_lr)}


def reference(x, weight_words, weight_scales, low_rank_weight):
    x = f64(x)
    w_lr = f64(low_rank_weight)
    r = w_lr.shape[1]
    out = x[:, :r] @ w_lr.T
    w = unpack_weight(weight_words, weight_scales, "e4m3")
    out = out + (mxq(x, 1, "e4m3") @ w)
    return out

@@ -1,0 +1,246 @@
+from contextlib import ExitStack
+
+import concourse.mybir as mybir
+from concourse.masks import make_identity
+
+F32 = mybir.dt.float32
+BF16 = mybir.dt.bfloat16
+I32 = mybir.dt.int32
+U32 = mybir.dt.uint32
+U8 = mybir.dt.uint8
+FP8X4 = mybir.dt.float8_e4m3fn_x4
+ADD = mybir.AluOpType.add
+
+P = 128
+M, K, N, R = 256, 4096, 4096, 128
+M_TILES = M // P
+GROUPS = K // 512
+ROUNDS = 4
+ROUND_COLS = N // ROUNDS
+N_TILE = 512
+PIECES = 4
+
+FLOPS = 2 * M * K * N + 2 * M * R * N
+
+
+def tile_linear4bit_kernel(tc, x, weight_words, weight_scales, low_rank_weight, out):
+    nc = tc.nc
+    with ExitStack() as ctx:
+        keep = ctx.enter_context(tc.tile_pool(name="keep", bufs=1))
+        big = ctx.enter_context(tc.tile_pool(name="big", bufs=16))
+        psum = ctx.enter_context(tc.psum_pool(name="psum", bufs=1))
+        ctx.enter_context(tc.manual_schedule())
+
+        used_banks = []
+
+        def next_bank(shape, dtype, name):
+            tag = "bank%d" % (len(used_banks) % 8)
+            used_banks.append(tag)
+            return psum.tile(shape, dtype, tag=tag, name=name)
+
+        planes_w = []
+        for a in range(2):
+            t = keep.tile([P, N], U8, name="planes_w%d" % a, align_bytes=64)
+            nc.vector.memset(t[:].bitcast(I32), 0)
+            planes_w.append(t)
+        warm_in = keep.tile([P, 8], F32, name="warm_in")
+        nc.vector.memset(warm_in[:], 0.0)
+        warm_out = keep.tile([P, 8], F32, name="warm_out")
+        nc.scalar.copy(out=warm_out[:], in_=warm_in[:])
+
+        ident_b = keep.tile([P, P], BF16, name="ident_b")
+        make_identity(nc, ident_b[:])
+        ident_f = keep.tile([P, P], F32, name="ident_f")
+        make_identity(nc, ident_f[:])
+
+        xlr = keep.tile([P, M_TILES, P], BF16, name="xlr")
+        nc.sync.dma_start(out=xlr[:], in_=x[:, 0:R].rearrange("(t p) r -> p t r", p=P))
+        wl = []
+        for c in range(ROUNDS):
+            t = keep.tile([P, 8, R], BF16, name="wl%d" % c)
+            nc.sync.dma_start(
+                out=t[:],
+                in_=low_rank_weight[ROUND_COLS * c : ROUND_COLS * (c + 1), :].rearrange(
+                    "(p j) r -> p j r", j=8
+                ),
+            )
+            wl.append(t)
+        x_raw = []
+        for mt in range(M_TILES):
+            t = big.tile([P, K], BF16, tag="big", name="x_raw%d" % mt, align_bytes=64)
+            nc.sync.dma_start(out=t[:], in_=x[mt * P : (mt + 1) * P, :])
+            x_raw.append(t)
+
+        for a in range(2):
+            for q in (0, 2, 1, 3):
+                nc.sync.dma_start(
+                    out=planes_w[a][32 * q : 32 * q + 16, :].bitcast(I32),
+                    in_=weight_scales[4 * a : 4 * a + 4, 4 * q : 4 * q + 4, :].bitcast(I32),
+                )
+
+        words = weight_words.rearrange("g p n t -> p g (n t)")
+        w_tiles = []
+
+        def load_piece(i):
+            c, s = divmod(i, PIECES)
+            t = big.tile([P, 2, ROUND_COLS], U32, tag="big", name="w%d" % i, align_bytes=64)
+            nc.sync.dma_start(
+                out=t[:].bitcast(I32),
+                in_=words[
+                    :, 2 * s : 2 * s + 2, 4 * ROUND_COLS * c : 4 * ROUND_COLS * (c + 1)
+                ].bitcast(I32),
+            )
+            w_tiles.append(t)
+
+        for i in range(14):
+            load_piece(i)
+
+        xlr_ps = next_bank([P, M_TILES, P], BF16, "xlr_ps")
+        for mt in range(M_TILES):
+            nc.tensor.transpose(xlr_ps[:, mt, :], xlr[:, mt, :], ident_b[:])
+        xlrT = keep.tile([P, M_TILES, P], BF16, name="xlrT")
+        nc.scalar.copy(out=xlrT[:], in_=xlr_ps[:])
+
+        wT = []
+
+        def transpose_wl(c):
+            ps = next_bank([P, 8, P], BF16, "wl_ps")
+            for j in range(8):
+                nc.tensor.transpose(ps[:, j, :], wl[c][:, j, :], ident_b[:])
+            t = keep.tile([P, 8 * P], BF16, name="wT%d" % c)
+            nc.scalar.copy(out=t[:], in_=ps[:].rearrange("r j p -> r (j p)"))
+            wT.append(t)
+
+        res = [
+            [keep.tile([P, ROUND_COLS], F32, name="res%d_%d" % (c, mt)) for mt in range(M_TILES)]
+            for c in range(ROUNDS)
+        ]
+
+        def low_rank(c, mt, jh, engine):
+            ps = next_bank([P, N_TILE], F32, "lr_ps")
+            nc.tensor.matmul(
+                ps[:],
+                lhsT=xlrT[:, mt, :],
+                rhs=wT[c][:, N_TILE * jh : N_TILE * (jh + 1)],
+                start=True,
+                stop=True,
+            )
+            dst = res[c][mt][:].rearrange("m (p j) -> m p j", j=8)[:, :, 4 * jh : 4 * jh + 4]
+            src = ps[:].rearrange("m (j p) -> m p j", j=4)
+            if engine == "v":
+                nc.vector.tensor_copy(out=dst, in_=src)
+            else:
+                nc.scalar.copy(out=dst, in_=src)
+
+        def low_rank_round(c):
+            low_rank(c, 0, 0, "v")
+            low_rank(c, 1, 0, "s")
+            low_rank(c, 0, 1, "v")
+            low_rank(c, 1, 1, "s")
+
+        transpose_wl(0)
+        transpose_wl(1)
+        low_rank_round(0)
+        transpose_wl(2)
+        low_rank_round(1)
+        transpose_wl(3)
+        low_rank_round(2)
+
+        grouped = [
+            [
+                keep.tile([P, 4, P, 4], BF16, name="grouped%d_%d" % (mt, h), align_bytes=64)
+                for h in range(2)
+            ]
+            for mt in range(M_TILES)
+        ]
+        codes = [
+            [
+                keep.tile([P, 4, P], U32, name="codes%d_%d" % (mt, h), align_bytes=64)
+                for h in range(2)
+            ]
+            for mt in range(M_TILES)
+        ]
+        planes_x = [
+            [
+                keep.tile([P, 4, P], U8, name="planes_x%d_%d" % (mt, h), align_bytes=64)
+                for h in range(2)
+            ]
+            for mt in range(M_TILES)
+        ]
+
+        def transpose_x(mt, b, engine):
+            ps = next_bank([P, 4, P], F32, "x_ps")
+            xw = x_raw[mt][:].bitcast(F32)
+            for gi in range(2):
+                g = 2 * b + gi
+                for u in range(2):
+                    nc.tensor.transpose(
+                        ps[:, 2 * gi + u, :], xw[:, 256 * g + u : 256 * (g + 1) : 2], ident_f[:]
+                    )
+            h, b2 = divmod(b, 2)
+            dst = grouped[mt][h][:].bitcast(F32)[:, 2 * b2 : 2 * b2 + 2, :, :]
+            src = ps[:].rearrange("p (g u) m -> p g m u", u=2)
+            if engine == "v":
+                nc.vector.tensor_copy(out=dst, in_=src)
+            else:
+                nc.scalar.copy(out=dst, in_=src)
+
+        def quantise(mt, h):
+            nc.vector.quantize_mx(
+                out=codes[mt][h][:].rearrange("p g m -> p (g m)").bitcast(FP8X4),
+                scales=planes_x[mt][h][:].rearrange("p g m -> p (g m)"),
+                in_=grouped[mt][h][:].rearrange("p g m t -> p (g m t)"),
+            )
+
+        transpose_x(0, 0, "v")
+        transpose_x(0, 1, "s")
+        transpose_x(0, 2, "v")
+        transpose_x(0, 3, "s")
+        quantise(0, 0)
+        low_rank(3, 0, 0, "s")
+        low_rank(3, 0, 1, "s")
+        quantise(0, 1)
+        transpose_x(1, 0, "v")
+        transpose_x(1, 1, "s")
+        quantise(1, 0)
+        transpose_x(1, 2, "v")
+        transpose_x(1, 3, "s")
+        low_rank(3, 1, 0, "s")
+        low_rank(3, 1, 1, "s")
+        quantise(1, 1)
+
+        load_piece(14)
+        load_piece(15)
+
+        for c in range(ROUNDS):
+            acc = {}
+            for mt in range(M_TILES):
+                for nt in range(2):
+                    acc[(mt, nt)] = next_bank([P, N_TILE], F32, "acc")
+            for s in range(PIECES):
+                wt = w_tiles[PIECES * c + s]
+                if s < PIECES - 1:
+                    order = [(gi, mt, nt) for gi in range(2) for nt in range(2) for mt in range(2)]
+                else:
+                    order = [(gi, mt, nt) for mt in range(2) for nt in range(2) for gi in range(2)]
+                for gi, mt, nt in order:
+                    g = 2 * s + gi
+                    a, j = divmod(g, 4)
+                    col = ROUND_COLS * c + N_TILE * nt
+                    nc.tensor.matmul_mx(
+                        out=acc[(mt, nt)][:],
+                        lhsT=codes[mt][a][:, j, :].bitcast(FP8X4),
+                        lhsT_scale=planes_x[mt][a][:, j, :],
+                        rhs=wt[:, gi, N_TILE * nt : N_TILE * (nt + 1)].bitcast(FP8X4),
+                        rhs_scale=planes_w[a][4 * j : P, col : col + N_TILE],
+                        start=(g == 0),
+                        stop=(g == GROUPS - 1),
+                    )
+            for mt in range(M_TILES):
+                for nt in range(2):
+                    part = res[c][mt][:, N_TILE * nt : N_TILE * (nt + 1)]
+                    nc.vector.tensor_tensor(out=part, in0=acc[(mt, nt)][:], in1=part, op=ADD)
+                nc.sync.dma_start(
+                    out=out[mt * P : (mt + 1) * P, ROUND_COLS * c : ROUND_COLS * (c + 1)],
+                    in_=res[c][mt][:],
+                )

@@ -73,9 +73,9 @@ def tile_linear4bit_kernel(tc, x, weight_words, weight_scales, low_rank_weight, 
 
         for a in range(2):
             for q in (0, 2, 1, 3):
-                nc.sync.dma_start(
-                    out=planes_w[a][32 * q : 32 * q + 16, :].bitcast(I32),
-                    in_=weight_scales[4 * a : 4 * a + 4, 4 * q : 4 * q + 4, :].bitcast(I32),
+                nc.gpsimd.dma_start(
+                    out=planes_w[a][32 * q : 32 * q + 16, :].bitcast(F32),
+                    in_=weight_scales[4 * a : 4 * a + 4, 4 * q : 4 * q + 4, :].bitcast(F32),
                 )
 
         words = weight_words.rearrange("g p n t -> p g (n t)")

@@ -19,6 +19,7 @@ ROUNDS = 4
 ROUND_COLS = N // ROUNDS
 N_TILE = 512
 PIECES = 4
+WARM_UP = 4
 
 FLOPS = 2 * M * K * N + 2 * M * R * N
 
@@ -37,6 +38,12 @@ def tile_linear4bit_kernel(tc, x, weight_words, weight_scales, low_rank_weight, 
             tag = "bank%d" % (len(used_banks) % 8)
             used_banks.append(tag)
             return psum.tile(shape, dtype, tag=tag, name=name)
+
+        zeros = keep.tile([P, N_TILE], BF16, name="zeros")
+        nc.vector.memset(zeros[:], 0.0)
+        idle_ps = next_bank([P, N_TILE], F32, "idle_ps")
+        for i in range(WARM_UP):
+            nc.tensor.matmul(idle_ps[:], lhsT=zeros[:, 0:P], rhs=zeros[:], start=True, stop=True)
 
         planes_w = []
         for a in range(2):
@@ -144,7 +151,6 @@ def tile_linear4bit_kernel(tc, x, weight_words, weight_scales, low_rank_weight, 
         transpose_wl(2)
         low_rank_round(1)
         transpose_wl(3)
-        low_rank_round(2)
 
         grouped = [
             [
@@ -193,19 +199,23 @@ def tile_linear4bit_kernel(tc, x, weight_words, weight_scales, low_rank_weight, 
             )
 
         transpose_x(0, 0, "v")
+        low_rank(2, 0, 0, "s")
         transpose_x(0, 1, "s")
+        low_rank(2, 0, 1, "s")
         transpose_x(0, 2, "v")
-        transpose_x(0, 3, "s")
         quantise(0, 0)
-        low_rank(3, 0, 0, "s")
-        low_rank(3, 0, 1, "s")
+        low_rank(2, 1, 0, "v")
+        transpose_x(0, 3, "s")
+        low_rank(2, 1, 1, "v")
         quantise(0, 1)
         transpose_x(1, 0, "v")
+        low_rank(3, 0, 0, "s")
         transpose_x(1, 1, "s")
         quantise(1, 0)
+        low_rank(3, 0, 1, "s")
         transpose_x(1, 2, "v")
-        transpose_x(1, 3, "s")
         low_rank(3, 1, 0, "s")
+        transpose_x(1, 3, "s")
         low_rank(3, 1, 1, "s")
         quantise(1, 1)
 

@@ -15,11 +15,14 @@ P = 128
 M, K, N, R = 256, 4096, 4096, 128
 M_TILES = M // P
 GROUPS = K // 512
-ROUNDS = 4
+ROUNDS = 2
 ROUND_COLS = N // ROUNDS
 N_TILE = 512
-PIECES = 4
+N_TILES = ROUND_COLS // N_TILE
+LR_BLOCKS = 4
+LR_COLS = N // LR_BLOCKS
 WARM_UP = 4
+SCALES_ON_GPSIMD = True
 
 FLOPS = 2 * M * K * N + 2 * M * R * N
 
@@ -63,11 +66,11 @@ def tile_linear4bit_kernel(tc, x, weight_words, weight_scales, low_rank_weight, 
         xlr = keep.tile([P, M_TILES, P], BF16, name="xlr")
         nc.sync.dma_start(out=xlr[:], in_=x[:, 0:R].rearrange("(t p) r -> p t r", p=P))
         wl = []
-        for c in range(ROUNDS):
-            t = keep.tile([P, 8, R], BF16, name="wl%d" % c)
+        for b in range(LR_BLOCKS):
+            t = keep.tile([P, 8, R], BF16, name="wl%d" % b)
             nc.sync.dma_start(
                 out=t[:],
-                in_=low_rank_weight[ROUND_COLS * c : ROUND_COLS * (c + 1), :].rearrange(
+                in_=low_rank_weight[LR_COLS * b : LR_COLS * (b + 1), :].rearrange(
                     "(p j) r -> p j r", j=8
                 ),
             )
@@ -80,22 +83,22 @@ def tile_linear4bit_kernel(tc, x, weight_words, weight_scales, low_rank_weight, 
 
         for a in range(2):
             for q in (0, 2, 1, 3):
-                nc.gpsimd.dma_start(
-                    out=planes_w[a][32 * q : 32 * q + 16, :].bitcast(F32),
-                    in_=weight_scales[4 * a : 4 * a + 4, 4 * q : 4 * q + 4, :].bitcast(F32),
-                )
+                dst = planes_w[a][32 * q : 32 * q + 16, :]
+                src = weight_scales[4 * a : 4 * a + 4, 4 * q : 4 * q + 4, :]
+                if SCALES_ON_GPSIMD:
+                    nc.gpsimd.dma_start(out=dst.bitcast(F32), in_=src.bitcast(F32))
+                else:
+                    nc.sync.dma_start(out=dst.bitcast(I32), in_=src.bitcast(I32))
 
         words = weight_words.rearrange("g p n t -> p g (n t)")
         w_tiles = []
 
         def load_piece(i):
-            c, s = divmod(i, PIECES)
-            t = big.tile([P, 2, ROUND_COLS], U32, tag="big", name="w%d" % i, align_bytes=64)
+            c, g = divmod(i, GROUPS)
+            t = big.tile([P, ROUND_COLS], U32, tag="big", name="w%d" % i, align_bytes=64)
             nc.sync.dma_start(
                 out=t[:].bitcast(I32),
-                in_=words[
-                    :, 2 * s : 2 * s + 2, 4 * ROUND_COLS * c : 4 * ROUND_COLS * (c + 1)
-                ].bitcast(I32),
+                in_=words[:, g, 4 * ROUND_COLS * c : 4 * ROUND_COLS * (c + 1)].bitcast(I32),
             )
             w_tiles.append(t)
 
@@ -110,11 +113,11 @@ def tile_linear4bit_kernel(tc, x, weight_words, weight_scales, low_rank_weight, 
 
         wT = []
 
-        def transpose_wl(c):
+        def transpose_wl(b):
             ps = next_bank([P, 8, P], BF16, "wl_ps")
             for j in range(8):
-                nc.tensor.transpose(ps[:, j, :], wl[c][:, j, :], ident_b[:])
-            t = keep.tile([P, 8 * P], BF16, name="wT%d" % c)
+                nc.tensor.transpose(ps[:, j, :], wl[b][:, j, :], ident_b[:])
+            t = keep.tile([P, 8 * P], BF16, name="wT%d" % b)
             nc.scalar.copy(out=t[:], in_=ps[:].rearrange("r j p -> r (j p)"))
             wT.append(t)
 
@@ -123,33 +126,35 @@ def tile_linear4bit_kernel(tc, x, weight_words, weight_scales, low_rank_weight, 
             for c in range(ROUNDS)
         ]
 
-        def low_rank(c, mt, jh, engine):
+        def low_rank(b, mt, jh, engine):
             ps = next_bank([P, N_TILE], F32, "lr_ps")
             nc.tensor.matmul(
                 ps[:],
                 lhsT=xlrT[:, mt, :],
-                rhs=wT[c][:, N_TILE * jh : N_TILE * (jh + 1)],
+                rhs=wT[b][:, N_TILE * jh : N_TILE * (jh + 1)],
                 start=True,
                 stop=True,
             )
-            dst = res[c][mt][:].rearrange("m (p j) -> m p j", j=8)[:, :, 4 * jh : 4 * jh + 4]
+            c, half = divmod(b, 2)
+            block = res[c][mt][:, LR_COLS * half : LR_COLS * (half + 1)]
+            dst = block.rearrange("m (p j) -> m p j", j=8)[:, :, 4 * jh : 4 * jh + 4]
             src = ps[:].rearrange("m (j p) -> m p j", j=4)
             if engine == "v":
                 nc.vector.tensor_copy(out=dst, in_=src)
             else:
                 nc.scalar.copy(out=dst, in_=src)
 
-        def low_rank_round(c):
-            low_rank(c, 0, 0, "v")
-            low_rank(c, 1, 0, "s")
-            low_rank(c, 0, 1, "v")
-            low_rank(c, 1, 1, "s")
+        def low_rank_block(b):
+            low_rank(b, 0, 0, "v")
+            low_rank(b, 1, 0, "s")
+            low_rank(b, 0, 1, "v")
+            low_rank(b, 1, 1, "s")
 
         transpose_wl(0)
         transpose_wl(1)
-        low_rank_round(0)
+        low_rank_block(0)
         transpose_wl(2)
-        low_rank_round(1)
+        low_rank_block(1)
         transpose_wl(3)
 
         grouped = [
@@ -222,35 +227,38 @@ def tile_linear4bit_kernel(tc, x, weight_words, weight_scales, low_rank_weight, 
         load_piece(14)
         load_piece(15)
 
+        out_tiles = [(mt, nt) for mt in range(M_TILES) for nt in range(N_TILES)]
         for c in range(ROUNDS):
             acc = {}
-            for mt in range(M_TILES):
-                for nt in range(2):
-                    acc[(mt, nt)] = next_bank([P, N_TILE], F32, "acc")
-            for s in range(PIECES):
-                wt = w_tiles[PIECES * c + s]
-                if s < PIECES - 1:
-                    order = [(gi, mt, nt) for gi in range(2) for nt in range(2) for mt in range(2)]
-                else:
-                    order = [(gi, mt, nt) for mt in range(2) for nt in range(2) for gi in range(2)]
-                for gi, mt, nt in order:
-                    g = 2 * s + gi
-                    a, j = divmod(g, 4)
-                    col = ROUND_COLS * c + N_TILE * nt
-                    nc.tensor.matmul_mx(
-                        out=acc[(mt, nt)][:],
-                        lhsT=codes[mt][a][:, j, :].bitcast(FP8X4),
-                        lhsT_scale=planes_x[mt][a][:, j, :],
-                        rhs=wt[:, gi, N_TILE * nt : N_TILE * (nt + 1)].bitcast(FP8X4),
-                        rhs_scale=planes_w[a][4 * j : P, col : col + N_TILE],
-                        start=(g == 0),
-                        stop=(g == GROUPS - 1),
-                    )
-            for mt in range(M_TILES):
-                for nt in range(2):
-                    part = res[c][mt][:, N_TILE * nt : N_TILE * (nt + 1)]
-                    nc.vector.tensor_tensor(out=part, in0=acc[(mt, nt)][:], in1=part, op=ADD)
-                nc.sync.dma_start(
-                    out=out[mt * P : (mt + 1) * P, ROUND_COLS * c : ROUND_COLS * (c + 1)],
-                    in_=res[c][mt][:],
+            for key in out_tiles:
+                acc[key] = next_bank([P, N_TILE], F32, "acc")
+
+            def mx_pass(g, mt, nt):
+                a, j = divmod(g, 4)
+                col = ROUND_COLS * c + N_TILE * nt
+                nc.tensor.matmul_mx(
+                    out=acc[(mt, nt)][:],
+                    lhsT=codes[mt][a][:, j, :].bitcast(FP8X4),
+                    lhsT_scale=planes_x[mt][a][:, j, :],
+                    rhs=w_tiles[GROUPS * c + g][:, N_TILE * nt : N_TILE * (nt + 1)].bitcast(FP8X4),
+                    rhs_scale=planes_w[a][4 * j : P, col : col + N_TILE],
+                    start=(g == 0),
+                    stop=(g == GROUPS - 1),
                 )
+
+            for g in range(GROUPS - 2):
+                for mt, nt in out_tiles:
+                    mx_pass(g, mt, nt)
+            for mt, nt in out_tiles:
+                mx_pass(GROUPS - 2, mt, nt)
+                mx_pass(GROUPS - 1, mt, nt)
+                part = res[c][mt][:, N_TILE * nt : N_TILE * (nt + 1)]
+                nc.vector.tensor_tensor(out=part, in0=acc[(mt, nt)][:], in1=part, op=ADD)
+                rows = out[mt * P : (mt + 1) * P, ROUND_COLS * c : ROUND_COLS * (c + 1)]
+                if c < ROUNDS - 1:
+                    if nt == N_TILES - 1:
+                        nc.sync.dma_start(out=rows, in_=res[c][mt][:])
+                elif nt % 2 == 1:
+                    lo = N_TILE * (nt - 1)
+                    hi = N_TILE * (nt + 1)
+                    nc.sync.dma_start(out=rows[:, lo:hi], in_=res[c][mt][:, lo:hi])

@@ -65,19 +65,15 @@ def tile_linear4bit_kernel(tc, x, weight_words, weight_scales, low_rank_weight, 
 
         xlr = keep.tile([P, M_TILES, P], BF16, name="xlr")
         nc.sync.dma_start(out=xlr[:], in_=x[:, 0:R].rearrange("(t p) r -> p t r", p=P))
+        wl_rows = low_rank_weight.rearrange("(b p j) r -> p b (j r)", b=LR_BLOCKS, j=8)
         wl = []
-        for b in range(LR_BLOCKS):
-            t = keep.tile([P, 8, R], BF16, name="wl%d" % b)
-            nc.sync.dma_start(
-                out=t[:],
-                in_=low_rank_weight[LR_COLS * b : LR_COLS * (b + 1), :].rearrange(
-                    "(p j) r -> p j r", j=8
-                ),
-            )
+        for half in range(2):
+            t = keep.tile([P, 2, 8 * R], BF16, name="wl%d" % half)
+            nc.sync.dma_start(out=t[:], in_=wl_rows[:, 2 * half : 2 * half + 2, :])
             wl.append(t)
         x_raw = []
         for mt in range(M_TILES):
-            t = big.tile([P, K], BF16, tag="big", name="x_raw%d" % mt, align_bytes=64)
+            t = big.tile([P, K], BF16, tag="one", bufs=2, name="x_raw%d" % mt, align_bytes=64)
             nc.sync.dma_start(out=t[:], in_=x[mt * P : (mt + 1) * P, :])
             x_raw.append(t)
 
@@ -91,19 +87,29 @@ def tile_linear4bit_kernel(tc, x, weight_words, weight_scales, low_rank_weight, 
                     nc.sync.dma_start(out=dst.bitcast(I32), in_=src.bitcast(I32))
 
         words = weight_words.rearrange("g p n t -> p g (n t)")
-        w_tiles = []
+        w_views = []
 
-        def load_piece(i):
+        def load_two_groups(i):
+            c, g = divmod(2 * i, GROUPS)
+            t = big.tile([P, 2, ROUND_COLS], U32, tag="two", bufs=7, name="w2_%d" % i, align_bytes=64)
+            nc.sync.dma_start(
+                out=t[:].bitcast(I32),
+                in_=words[:, g : g + 2, 4 * ROUND_COLS * c : 4 * ROUND_COLS * (c + 1)].bitcast(I32),
+            )
+            w_views.append(t[:, 0, :])
+            w_views.append(t[:, 1, :])
+
+        def load_one_group(i):
             c, g = divmod(i, GROUPS)
-            t = big.tile([P, ROUND_COLS], U32, tag="big", name="w%d" % i, align_bytes=64)
+            t = big.tile([P, ROUND_COLS], U32, tag="one", bufs=2, name="w1_%d" % i, align_bytes=64)
             nc.sync.dma_start(
                 out=t[:].bitcast(I32),
                 in_=words[:, g, 4 * ROUND_COLS * c : 4 * ROUND_COLS * (c + 1)].bitcast(I32),
             )
-            w_tiles.append(t)
+            w_views.append(t[:])
 
-        for i in range(14):
-            load_piece(i)
+        for i in range(7):
+            load_two_groups(i)
 
         xlr_ps = next_bank([P, M_TILES, P], BF16, "xlr_ps")
         for mt in range(M_TILES):
@@ -116,15 +122,14 @@ def tile_linear4bit_kernel(tc, x, weight_words, weight_scales, low_rank_weight, 
         def transpose_wl(b):
             ps = next_bank([P, 8, P], BF16, "wl_ps")
             for j in range(8):
-                nc.tensor.transpose(ps[:, j, :], wl[b][:, j, :], ident_b[:])
+                nc.tensor.transpose(
+                    ps[:, j, :], wl[b // 2][:, b % 2, R * j : R * (j + 1)], ident_b[:]
+                )
             t = keep.tile([P, 8 * P], BF16, name="wT%d" % b)
             nc.scalar.copy(out=t[:], in_=ps[:].rearrange("r j p -> r (j p)"))
             wT.append(t)
 
-        res = [
-            [keep.tile([P, ROUND_COLS], F32, name="res%d_%d" % (c, mt)) for mt in range(M_TILES)]
-            for c in range(ROUNDS)
-        ]
+        res = [keep.tile([P, M_TILES, ROUND_COLS], F32, name="res%d" % c) for c in range(ROUNDS)]
 
         def low_rank(b, mt, jh, engine):
             ps = next_bank([P, N_TILE], F32, "lr_ps")
@@ -136,7 +141,7 @@ def tile_linear4bit_kernel(tc, x, weight_words, weight_scales, low_rank_weight, 
                 stop=True,
             )
             c, half = divmod(b, 2)
-            block = res[c][mt][:, LR_COLS * half : LR_COLS * (half + 1)]
+            block = res[c][:, mt, LR_COLS * half : LR_COLS * (half + 1)]
             dst = block.rearrange("m (p j) -> m p j", j=8)[:, :, 4 * jh : 4 * jh + 4]
             src = ps[:].rearrange("m (j p) -> m p j", j=4)
             if engine == "v":
@@ -224,8 +229,8 @@ def tile_linear4bit_kernel(tc, x, weight_words, weight_scales, low_rank_weight, 
         low_rank(3, 1, 1, "s")
         quantise(1, 1)
 
-        load_piece(14)
-        load_piece(15)
+        load_one_group(14)
+        load_one_group(15)
 
         out_tiles = [(mt, nt) for mt in range(M_TILES) for nt in range(N_TILES)]
         for c in range(ROUNDS):
@@ -240,7 +245,7 @@ def tile_linear4bit_kernel(tc, x, weight_words, weight_scales, low_rank_weight, 
                     out=acc[(mt, nt)][:],
                     lhsT=codes[mt][a][:, j, :].bitcast(FP8X4),
                     lhsT_scale=planes_x[mt][a][:, j, :],
-                    rhs=w_tiles[GROUPS * c + g][:, N_TILE * nt : N_TILE * (nt + 1)].bitcast(FP8X4),
+                    rhs=w_views[GROUPS * c + g][:, N_TILE * nt : N_TILE * (nt + 1)].bitcast(FP8X4),
                     rhs_scale=planes_w[a][4 * j : P, col : col + N_TILE],
                     start=(g == 0),
                     stop=(g == GROUPS - 1),
@@ -252,13 +257,19 @@ def tile_linear4bit_kernel(tc, x, weight_words, weight_scales, low_rank_weight, 
             for mt, nt in out_tiles:
                 mx_pass(GROUPS - 2, mt, nt)
                 mx_pass(GROUPS - 1, mt, nt)
-                part = res[c][mt][:, N_TILE * nt : N_TILE * (nt + 1)]
+                part = res[c][:, mt, N_TILE * nt : N_TILE * (nt + 1)]
                 nc.vector.tensor_tensor(out=part, in0=acc[(mt, nt)][:], in1=part, op=ADD)
                 rows = out[mt * P : (mt + 1) * P, ROUND_COLS * c : ROUND_COLS * (c + 1)]
                 if c < ROUNDS - 1:
+                    if (mt, nt) == out_tiles[-1]:
+                        nc.sync.dma_start(
+                            out=out.rearrange("(t p) n -> p t n", p=P)[:, :, 0:ROUND_COLS],
+                            in_=res[c][:],
+                        )
+                elif mt == 0:
                     if nt == N_TILES - 1:
-                        nc.sync.dma_start(out=rows, in_=res[c][mt][:])
+                        nc.sync.dma_start(out=rows, in_=res[c][:, mt, :])
                 elif nt % 2 == 1:
                     lo = N_TILE * (nt - 1)
                     hi = N_TILE * (nt + 1)
-                    nc.sync.dma_start(out=rows[:, lo:hi], in_=res[c][mt][:, lo:hi])
+                    nc.sync.dma_start(out=rows[:, lo:hi], in_=res[c][:, mt, lo:hi])

@@ -19,6 +19,7 @@ ROUNDS = 2
 ROUND_COLS = N // ROUNDS
 N_TILE = 512
 N_TILES = ROUND_COLS // N_TILE
+HALF_COLS = ROUND_COLS // 2
 LR_BLOCKS = 4
 LR_COLS = N // LR_BLOCKS
 WARM_UP = 4
@@ -65,15 +66,19 @@ def tile_linear4bit_kernel(tc, x, weight_words, weight_scales, low_rank_weight, 
 
         xlr = keep.tile([P, M_TILES, P], BF16, name="xlr")
         nc.sync.dma_start(out=xlr[:], in_=x[:, 0:R].rearrange("(t p) r -> p t r", p=P))
-        wl_rows = low_rank_weight.rearrange("(b p j) r -> p b (j r)", b=LR_BLOCKS, j=8)
         wl = []
-        for half in range(2):
-            t = keep.tile([P, 2, 8 * R], BF16, name="wl%d" % half)
-            nc.sync.dma_start(out=t[:], in_=wl_rows[:, 2 * half : 2 * half + 2, :])
+        for b in range(LR_BLOCKS):
+            t = keep.tile([P, 8, R], BF16, name="wl%d" % b)
+            nc.sync.dma_start(
+                out=t[:],
+                in_=low_rank_weight[LR_COLS * b : LR_COLS * (b + 1), :].rearrange(
+                    "(p j) r -> p j r", j=8
+                ),
+            )
             wl.append(t)
         x_raw = []
         for mt in range(M_TILES):
-            t = big.tile([P, K], BF16, tag="one", bufs=2, name="x_raw%d" % mt, align_bytes=64)
+            t = big.tile([P, K], BF16, tag="big", name="x_raw%d" % mt, align_bytes=64)
             nc.sync.dma_start(out=t[:], in_=x[mt * P : (mt + 1) * P, :])
             x_raw.append(t)
 
@@ -87,29 +92,29 @@ def tile_linear4bit_kernel(tc, x, weight_words, weight_scales, low_rank_weight, 
                     nc.sync.dma_start(out=dst.bitcast(I32), in_=src.bitcast(I32))
 
         words = weight_words.rearrange("g p n t -> p g (n t)")
-        w_views = []
+        w_tiles = []
 
-        def load_two_groups(i):
-            c, g = divmod(2 * i, GROUPS)
-            t = big.tile([P, 2, ROUND_COLS], U32, tag="two", bufs=7, name="w2_%d" % i, align_bytes=64)
-            nc.sync.dma_start(
-                out=t[:].bitcast(I32),
-                in_=words[:, g : g + 2, 4 * ROUND_COLS * c : 4 * ROUND_COLS * (c + 1)].bitcast(I32),
-            )
-            w_views.append(t[:, 0, :])
-            w_views.append(t[:, 1, :])
-
-        def load_one_group(i):
+        def load_piece(i):
             c, g = divmod(i, GROUPS)
-            t = big.tile([P, ROUND_COLS], U32, tag="one", bufs=2, name="w1_%d" % i, align_bytes=64)
+            t = big.tile([P, ROUND_COLS], U32, tag="big", name="w%d" % i, align_bytes=64)
             nc.sync.dma_start(
                 out=t[:].bitcast(I32),
                 in_=words[:, g, 4 * ROUND_COLS * c : 4 * ROUND_COLS * (c + 1)].bitcast(I32),
             )
-            w_views.append(t[:])
+            w_tiles.append(t)
 
-        for i in range(7):
-            load_two_groups(i)
+        for i in range(14):
+            load_piece(i)
+
+        last = {}
+        for half in range(2):
+            for g in (GROUPS - 2, GROUPS - 1):
+                t = keep.tile([P, HALF_COLS], U32, name="last%d_%d" % (g, half), align_bytes=64)
+                lo = 4 * (ROUND_COLS * (ROUNDS - 1) + HALF_COLS * half)
+                nc.sync.dma_start(
+                    out=t[:].bitcast(I32), in_=words[:, g, lo : lo + 4 * HALF_COLS].bitcast(I32)
+                )
+                last[(g, half)] = t
 
         xlr_ps = next_bank([P, M_TILES, P], BF16, "xlr_ps")
         for mt in range(M_TILES):
@@ -122,14 +127,15 @@ def tile_linear4bit_kernel(tc, x, weight_words, weight_scales, low_rank_weight, 
         def transpose_wl(b):
             ps = next_bank([P, 8, P], BF16, "wl_ps")
             for j in range(8):
-                nc.tensor.transpose(
-                    ps[:, j, :], wl[b // 2][:, b % 2, R * j : R * (j + 1)], ident_b[:]
-                )
+                nc.tensor.transpose(ps[:, j, :], wl[b][:, j, :], ident_b[:])
             t = keep.tile([P, 8 * P], BF16, name="wT%d" % b)
             nc.scalar.copy(out=t[:], in_=ps[:].rearrange("r j p -> r (j p)"))
             wT.append(t)
 
-        res = [keep.tile([P, M_TILES, ROUND_COLS], F32, name="res%d" % c) for c in range(ROUNDS)]
+        res = [
+            [keep.tile([P, ROUND_COLS], F32, name="res%d_%d" % (c, mt)) for mt in range(M_TILES)]
+            for c in range(ROUNDS)
+        ]
 
         def low_rank(b, mt, jh, engine):
             ps = next_bank([P, N_TILE], F32, "lr_ps")
@@ -141,7 +147,7 @@ def tile_linear4bit_kernel(tc, x, weight_words, weight_scales, low_rank_weight, 
                 stop=True,
             )
             c, half = divmod(b, 2)
-            block = res[c][:, mt, LR_COLS * half : LR_COLS * (half + 1)]
+            block = res[c][mt][:, LR_COLS * half : LR_COLS * (half + 1)]
             dst = block.rearrange("m (p j) -> m p j", j=8)[:, :, 4 * jh : 4 * jh + 4]
             src = ps[:].rearrange("m (j p) -> m p j", j=4)
             if engine == "v":
@@ -229,10 +235,10 @@ def tile_linear4bit_kernel(tc, x, weight_words, weight_scales, low_rank_weight, 
         low_rank(3, 1, 1, "s")
         quantise(1, 1)
 
-        load_one_group(14)
-        load_one_group(15)
-
         out_tiles = [(mt, nt) for mt in range(M_TILES) for nt in range(N_TILES)]
+        by_halves = [
+            (mt, 2 * half + i) for half in range(2) for mt in range(M_TILES) for i in range(2)
+        ]
         for c in range(ROUNDS):
             acc = {}
             for key in out_tiles:
@@ -241,11 +247,16 @@ def tile_linear4bit_kernel(tc, x, weight_words, weight_scales, low_rank_weight, 
             def mx_pass(g, mt, nt):
                 a, j = divmod(g, 4)
                 col = ROUND_COLS * c + N_TILE * nt
+                if c == ROUNDS - 1 and g >= GROUPS - 2:
+                    half, i = divmod(nt, 2)
+                    moving = last[(g, half)][:, N_TILE * i : N_TILE * (i + 1)]
+                else:
+                    moving = w_tiles[GROUPS * c + g][:, N_TILE * nt : N_TILE * (nt + 1)]
                 nc.tensor.matmul_mx(
                     out=acc[(mt, nt)][:],
                     lhsT=codes[mt][a][:, j, :].bitcast(FP8X4),
                     lhsT_scale=planes_x[mt][a][:, j, :],
-                    rhs=w_views[GROUPS * c + g][:, N_TILE * nt : N_TILE * (nt + 1)].bitcast(FP8X4),
+                    rhs=moving.bitcast(FP8X4),
                     rhs_scale=planes_w[a][4 * j : P, col : col + N_TILE],
                     start=(g == 0),
                     stop=(g == GROUPS - 1),
@@ -254,22 +265,16 @@ def tile_linear4bit_kernel(tc, x, weight_words, weight_scales, low_rank_weight, 
             for g in range(GROUPS - 2):
                 for mt, nt in out_tiles:
                     mx_pass(g, mt, nt)
-            for mt, nt in out_tiles:
+            for mt, nt in out_tiles if c < ROUNDS - 1 else by_halves:
                 mx_pass(GROUPS - 2, mt, nt)
                 mx_pass(GROUPS - 1, mt, nt)
-                part = res[c][:, mt, N_TILE * nt : N_TILE * (nt + 1)]
+                part = res[c][mt][:, N_TILE * nt : N_TILE * (nt + 1)]
                 nc.vector.tensor_tensor(out=part, in0=acc[(mt, nt)][:], in1=part, op=ADD)
                 rows = out[mt * P : (mt + 1) * P, ROUND_COLS * c : ROUND_COLS * (c + 1)]
                 if c < ROUNDS - 1:
-                    if (mt, nt) == out_tiles[-1]:
-                        nc.sync.dma_start(
-                            out=out.rearrange("(t p) n -> p t n", p=P)[:, :, 0:ROUND_COLS],
-                            in_=res[c][:],
-                        )
-                elif mt == 0:
                     if nt == N_TILES - 1:
-                        nc.sync.dma_start(out=rows, in_=res[c][:, mt, :])
+                        nc.sync.dma_start(out=rows, in_=res[c][mt][:])
                 elif nt % 2 == 1:
                     lo = N_TILE * (nt - 1)
                     hi = N_TILE * (nt + 1)
-                    nc.sync.dma_start(out=rows[:, lo:hi], in_=res[c][:, mt, lo:hi])
+                    nc.sync.dma_start(out=rows[:, lo:hi], in_=res[c][mt][:, lo:hi])

@@ -22,7 +22,6 @@ N_TILES = ROUND_COLS // N_TILE
 HALF_COLS = ROUND_COLS // 2
 LR_BLOCKS = 4
 LR_COLS = N // LR_BLOCKS
-WARM_UP = 4
 SCALES_ON_GPSIMD = True
 
 FLOPS = 2 * M * K * N + 2 * M * R * N
@@ -42,12 +41,6 @@ def tile_linear4bit_kernel(tc, x, weight_words, weight_scales, low_rank_weight, 
             tag = "bank%d" % (len(used_banks) % 8)
             used_banks.append(tag)
             return psum.tile(shape, dtype, tag=tag, name=name)
-
-        zeros = keep.tile([P, N_TILE], BF16, name="zeros")
-        nc.vector.memset(zeros[:], 0.0)
-        idle_ps = next_bank([P, N_TILE], F32, "idle_ps")
-        for i in range(WARM_UP):
-            nc.tensor.matmul(idle_ps[:], lhsT=zeros[:, 0:P], rhs=zeros[:], start=True, stop=True)
 
         planes_w = []
         for a in range(2):

from contextlib import ExitStack

import concourse.mybir as mybir
from concourse.masks import make_identity

F32 = mybir.dt.float32
BF16 = mybir.dt.bfloat16
I32 = mybir.dt.int32
U32 = mybir.dt.uint32
U8 = mybir.dt.uint8
FP8X4 = mybir.dt.float8_e4m3fn_x4
ADD = mybir.AluOpType.add

P = 128
M, K, N, R = 256, 4096, 4096, 128
M_TILES = M // P
GROUPS = K // 512
ROUNDS = 2
ROUND_COLS = N // ROUNDS
N_TILE = 512
N_TILES = ROUND_COLS // N_TILE
HALF_COLS = ROUND_COLS // 2
LR_BLOCKS = 4
LR_COLS = N // LR_BLOCKS
SCALES_ON_GPSIMD = True

FLOPS = 2 * M * K * N + 2 * M * R * N


def tile_linear4bit_kernel(tc, x, weight_words, weight_scales, low_rank_weight, out):
    nc = tc.nc
    with ExitStack() as ctx:
        keep = ctx.enter_context(tc.tile_pool(name="keep", bufs=1))
        big = ctx.enter_context(tc.tile_pool(name="big", bufs=16))
        psum = ctx.enter_context(tc.psum_pool(name="psum", bufs=1))
        ctx.enter_context(tc.manual_schedule())

        used_banks = []

        def next_bank(shape, dtype, name):
            tag = "bank%d" % (len(used_banks) % 8)
            used_banks.append(tag)
            return psum.tile(shape, dtype, tag=tag, name=name)

        planes_w = []
        for a in range(2):
            t = keep.tile([P, N], U8, name="planes_w%d" % a, align_bytes=64)
            nc.vector.memset(t[:].bitcast(I32), 0)
            planes_w.append(t)
        warm_in = keep.tile([P, 8], F32, name="warm_in")
        nc.vector.memset(warm_in[:], 0.0)
        warm_out = keep.tile([P, 8], F32, name="warm_out")
        nc.scalar.copy(out=warm_out[:], in_=warm_in[:])

        ident_b = keep.tile([P, P], BF16, name="ident_b")
        make_identity(nc, ident_b[:])
        ident_f = keep.tile([P, P], F32, name="ident_f")
        make_identity(nc, ident_f[:])

        xlr = keep.tile([P, M_TILES, P], BF16, name="xlr")
        nc.sync.dma_start(out=xlr[:], in_=x[:, 0:R].rearrange("(t p) r -> p t r", p=P))
        wl = []
        for b in range(LR_BLOCKS):
            t = keep.tile([P, 8, R], BF16, name="wl%d" % b)
            nc.sync.dma_start(
                out=t[:],
                in_=low_rank_weight[LR_COLS * b : LR_COLS * (b + 1), :].rearrange(
                    "(p j) r -> p j r", j=8
                ),
            )
            wl.append(t)
        x_raw = []
        for mt in range(M_TILES):
            t = big.tile([P, K], BF16, tag="big", name="x_raw%d" % mt, align_bytes=64)
            nc.sync.dma_start(out=t[:], in_=x[mt * P : (mt + 1) * P, :])
            x_raw.append(t)

        for a in range(2):
            for q in (0, 2, 1, 3):
                dst = planes_w[a][32 * q : 32 * q + 16, :]
                src = weight_scales[4 * a : 4 * a + 4, 4 * q : 4 * q + 4, :]
                if SCALES_ON_GPSIMD:
                    nc.gpsimd.dma_start(out=dst.bitcast(F32), in_=src.bitcast(F32))
                else:
                    nc.sync.dma_start(out=dst.bitcast(I32), in_=src.bitcast(I32))

        words = weight_words.rearrange("g p n t -> p g (n t)")
        w_tiles = []

        def load_piece(i):
            c, g = divmod(i, GROUPS)
            t = big.tile([P, ROUND_COLS], U32, tag="big", name="w%d" % i, align_bytes=64)
            nc.sync.dma_start(
                out=t[:].bitcast(I32),
                in_=words[:, g, 4 * ROUND_COLS * c : 4 * ROUND_COLS * (c + 1)].bitcast(I32),
            )
            w_tiles.append(t)

        for i in range(14):
            load_piece(i)

        last = {}
        for half in range(2):
            for g in (GROUPS - 2, GROUPS - 1):
                t = keep.tile([P, HALF_COLS], U32, name="last%d_%d" % (g, half), align_bytes=64)
                lo = 4 * (ROUND_COLS * (ROUNDS - 1) + HALF_COLS * half)
                nc.sync.dma_start(
                    out=t[:].bitcast(I32), in_=words[:, g, lo : lo + 4 * HALF_COLS].bitcast(I32)
                )
                last[(g, half)] = t

        xlr_ps = next_bank([P, M_TILES, P], BF16, "xlr_ps")
        for mt in range(M_TILES):
            nc.tensor.transpose(xlr_ps[:, mt, :], xlr[:, mt, :], ident_b[:])
        xlrT = keep.tile([P, M_TILES, P], BF16, name="xlrT")
        nc.scalar.copy(out=xlrT[:], in_=xlr_ps[:])

        wT = []

        def transpose_wl(b):
            ps = next_bank([P, 8, P], BF16, "wl_ps")
            for j in range(8):
                nc.tensor.transpose(ps[:, j, :], wl[b][:, j, :], ident_b[:])
            t = keep.tile([P, 8 * P], BF16, name="wT%d" % b)
            nc.scalar.copy(out=t[:], in_=ps[:].rearrange("r j p -> r (j p)"))
            wT.append(t)

        res = [
            [keep.tile([P, ROUND_COLS], F32, name="res%d_%d" % (c, mt)) for mt in range(M_TILES)]
            for c in range(ROUNDS)
        ]

        def low_rank(b, mt, jh, engine):
            ps = next_bank([P, N_TILE], F32, "lr_ps")
            nc.tensor.matmul(
                ps[:],
                lhsT=xlrT[:, mt, :],
                rhs=wT[b][:, N_TILE * jh : N_TILE * (jh + 1)],
                start=True,
                stop=True,
            )
            c, half = divmod(b, 2)
            block = res[c][mt][:, LR_COLS * half : LR_COLS * (half + 1)]
            dst = block.rearrange("m (p j) -> m p j", j=8)[:, :, 4 * jh : 4 * jh + 4]
            src = ps[:].rearrange("m (j p) -> m p j", j=4)
            if engine == "v":
                nc.vector.tensor_copy(out=dst, in_=src)
            else:
                nc.scalar.copy(out=dst, in_=src)

        def low_rank_block(b):
            low_rank(b, 0, 0, "v")
            low_rank(b, 1, 0, "s")
            low_rank(b, 0, 1, "v")
            low_rank(b, 1, 1, "s")

        transpose_wl(0)
        transpose_wl(1)
        low_rank_block(0)
        transpose_wl(2)
        low_rank_block(1)
        transpose_wl(3)

        grouped = [
            [
                keep.tile([P, 4, P, 4], BF16, name="grouped%d_%d" % (mt, h), align_bytes=64)
                for h in range(2)
            ]
            for mt in range(M_TILES)
        ]
        codes = [
            [
                keep.tile([P, 4, P], U32, name="codes%d_%d" % (mt, h), align_bytes=64)
                for h in range(2)
            ]
            for mt in range(M_TILES)
        ]
        planes_x = [
            [
                keep.tile([P, 4, P], U8, name="planes_x%d_%d" % (mt, h), align_bytes=64)
                for h in range(2)
            ]
            for mt in range(M_TILES)
        ]

        def transpose_x(mt, b, engine):
            ps = next_bank([P, 4, P], F32, "x_ps")
            xw = x_raw[mt][:].bitcast(F32)
            for gi in range(2):
                g = 2 * b + gi
                for u in range(2):
                    nc.tensor.transpose(
                        ps[:, 2 * gi + u, :], xw[:, 256 * g + u : 256 * (g + 1) : 2], ident_f[:]
                    )
            h, b2 = divmod(b, 2)
            dst = grouped[mt][h][:].bitcast(F32)[:, 2 * b2 : 2 * b2 + 2, :, :]
            src = ps[:].rearrange("p (g u) m -> p g m u", u=2)
            if engine == "v":
                nc.vector.tensor_copy(out=dst, in_=src)
            else:
                nc.scalar.copy(out=dst, in_=src)

        def quantise(mt, h):
            nc.vector.quantize_mx(
                out=codes[mt][h][:].rearrange("p g m -> p (g m)").bitcast(FP8X4),
                scales=planes_x[mt][h][:].rearrange("p g m -> p (g m)"),
                in_=grouped[mt][h][:].rearrange("p g m t -> p (g m t)"),
            )

        transpose_x(0, 0, "v")
        low_rank(2, 0, 0, "s")
        transpose_x(0, 1, "s")
        low_rank(2, 0, 1, "s")
        transpose_x(0, 2, "v")
        quantise(0, 0)
        low_rank(2, 1, 0, "v")
        transpose_x(0, 3, "s")
        low_rank(2, 1, 1, "v")
        quantise(0, 1)
        transpose_x(1, 0, "v")
        low_rank(3, 0, 0, "s")
        transpose_x(1, 1, "s")
        quantise(1, 0)
        low_rank(3, 0, 1, "s")
        transpose_x(1, 2, "v")
        low_rank(3, 1, 0, "s")
        transpose_x(1, 3, "s")
        low_rank(3, 1, 1, "s")
        quantise(1, 1)

        out_tiles = [(mt, nt) for mt in range(M_TILES) for nt in range(N_TILES)]
        by_halves = [
            (mt, 2 * half + i) for half in range(2) for mt in range(M_TILES) for i in range(2)
        ]
        for c in range(ROUNDS):
            acc = {}
            for key in out_tiles:
                acc[key] = next_bank([P, N_TILE], F32, "acc")

            def mx_pass(g, mt, nt):
                a, j = divmod(g, 4)
                col = ROUND_COLS * c + N_TILE * nt
                if c == ROUNDS - 1 and g >= GROUPS - 2:
                    half, i = divmod(nt, 2)
                    moving = last[(g, half)][:, N_TILE * i : N_TILE * (i + 1)]
                else:
                    moving = w_tiles[GROUPS * c + g][:, N_TILE * nt : N_TILE * (nt + 1)]
                nc.tensor.matmul_mx(
                    out=acc[(mt, nt)][:],
                    lhsT=codes[mt][a][:, j, :].bitcast(FP8X4),
                    lhsT_scale=planes_x[mt][a][:, j, :],
                    rhs=moving.bitcast(FP8X4),
                    rhs_scale=planes_w[a][4 * j : P, col : col + N_TILE],
                    start=(g == 0),
                    stop=(g == GROUPS - 1),
                )

            for g in range(GROUPS - 2):
                for mt, nt in out_tiles:
                    mx_pass(g, mt, nt)
            for mt, nt in out_tiles if c < ROUNDS - 1 else by_halves:
                mx_pass(GROUPS - 2, mt, nt)
                mx_pass(GROUPS - 1, mt, nt)
                part = res[c][mt][:, N_TILE * nt : N_TILE * (nt + 1)]
                nc.vector.tensor_tensor(out=part, in0=acc[(mt, nt)][:], in1=part, op=ADD)
                rows = out[mt * P : (mt + 1) * P, ROUND_COLS * c : ROUND_COLS * (c + 1)]
                if c < ROUNDS - 1:
                    if nt == N_TILES - 1:
                        nc.sync.dma_start(out=rows, in_=res[c][mt][:])
                elif nt % 2 == 1:
                    lo = N_TILE * (nt - 1)
                    hi = N_TILE * (nt + 1)
                    nc.sync.dma_start(out=rows[:, lo:hi], in_=res[c][mt][:, lo:hi])
